import numpy as np
import ml_dtypes

BF16 = ml_dtypes.bfloat16


def bf(x):
    return np.asarray(x, np.float32).astype(BF16)


def f32(x):
    return np.asarray(x, np.float32)


def f64(x):
    return np.asarray(x).astype(np.float64)


def striped(idx):
    return np.tile(idx.reshape(-1, 16).T, (8, 1))


C, S, M, F, K, H, N = 128, 512, 128, 512, 8, 256, 2048


def setup_inputs():
    idx = np.concatenate([np.random.permutation(S)[:H] for _ in range(K)])
    return {"x": f32(np.random.standard_normal((C, S))), "h_dst": f32(np.random.standard_normal((C, N))), "w1": bf(np.random.standard_normal((F, M)) / np.sqrt(F)), "b1": f32(0.1 * np.random.standard_normal((M, 1))), "offs": striped(idx)}


def reference(x, h_dst, w1, b1, offs):
    idx = offs[:16].T.reshape(-1)
    hi = f64(x)[:, idx]
    hd = f64(h_dst)
    feats = np.concatenate([hi, hd, np.abs(hi + (-hd)), hi * hd], axis=0)
    return np.maximum(f64(w1).T @ feats + f64(b1), 0.0)

@@ -1,0 +1,68 @@
+import concourse.mybir as mybir
+
+F32, BF16, U16 = mybir.dt.float32, mybir.dt.bfloat16, mybir.dt.uint16
+ADD, MULT = mybir.AluOpType.add, mybir.AluOpType.mult
+ACT = mybir.ActivationFunctionType
+
+P = 128
+NODES = 512
+EDGES = 2048
+BLOCKS = 4
+CHUNK = 512
+N_CHUNKS = EDGES // CHUNK
+OFFS_COLS = CHUNK // 16
+
+FLOPS = 2 * BLOCKS * P * P * EDGES
+
+
+def tile_stochasticrewiring_kernel(tc, x, h_dst, w1, b1, offs, out):
+    nc = tc.nc
+    with (
+        tc.tile_pool(name="held", bufs=1) as held,
+        tc.tile_pool(name="work", bufs=N_CHUNKS) as work,
+        tc.psum_pool(name="psum", bufs=N_CHUNKS) as psum,
+    ):
+        offsets = held.tile([P, EDGES // 16], U16, name="offsets")
+        nc.sync.dma_start(offsets[:], offs)
+        nodes = held.tile([P, NODES], F32, name="nodes")
+        nc.scalar.dma_start(nodes[:], x)
+        weights = held.tile([P, BLOCKS, P], BF16, name="weights")
+        nc.gpsimd.dma_start(weights[:], w1.rearrange("(b c) m -> c b m", c=P))
+        bias = held.tile([P, 1], F32, name="bias")
+        nc.gpsimd.dma_start(bias[:], b1)
+
+        for k in range(N_CHUNKS):
+            edges = slice(k * CHUNK, (k + 1) * CHUNK)
+            piece = offsets[:, k * OFFS_COLS : (k + 1) * OFFS_COLS]
+
+            dst = work.tile([P, CHUNK], F32, name="dst")
+            nc.sync.dma_start(dst[:], h_dst[:, edges])
+
+            neg_dst = work.tile([P, CHUNK], F32, name="neg_dst")
+            nc.gpsimd.tensor_scalar_mul(neg_dst[:], dst[:], -1.0)
+            dst_bf = work.tile([P, CHUNK], BF16, name="dst_bf")
+            nc.gpsimd.tensor_copy(dst_bf[:], dst[:])
+
+            src = work.tile([P, CHUNK], F32, name="src")
+            nc.vector.tensor_copy(src[:], nodes[:].indirect(piece))
+            prod = work.tile([P, CHUNK], F32, name="prod")
+            nc.vector.tensor_tensor(prod[:], nodes[:].indirect(piece), dst[:], MULT)
+            diff = work.tile([P, CHUNK], F32, name="diff")
+            nc.vector.tensor_tensor(diff[:], nodes[:].indirect(piece), neg_dst[:], ADD)
+
+            src_bf = work.tile([P, CHUNK], BF16, name="src_bf")
+            nc.scalar.activation(src_bf[:], src[:], ACT.Copy)
+            prod_bf = work.tile([P, CHUNK], BF16, name="prod_bf")
+            nc.scalar.activation(prod_bf[:], prod[:], ACT.Copy)
+            diff_bf = work.tile([P, CHUNK], BF16, name="diff_bf")
+            nc.scalar.activation(diff_bf[:], diff[:], ACT.Abs)
+
+            acc = psum.tile([P, CHUNK], F32, name="acc")
+            nc.tensor.matmul(acc[:], weights[:, 1, :], dst_bf[:], start=True, stop=False)
+            nc.tensor.matmul(acc[:], weights[:, 0, :], src_bf[:], start=False, stop=False)
+            nc.tensor.matmul(acc[:], weights[:, 3, :], prod_bf[:], start=False, stop=False)
+            nc.tensor.matmul(acc[:], weights[:, 2, :], diff_bf[:], start=False, stop=True)
+
+            hidden = work.tile([P, CHUNK], F32, name="hidden")
+            nc.scalar.activation(hidden[:], acc[:], ACT.Relu, bias=bias[:])
+            nc.sync.dma_start(out[:, edges], hidden[:])

@@ -27,28 +27,28 @@ def tile_stochasticrewiring_kernel(tc, x, h_dst, w1, b1, offs, out):
         nodes = held.tile([P, NODES], F32, name="nodes")
         nc.scalar.dma_start(nodes[:], x)
         weights = held.tile([P, BLOCKS, P], BF16, name="weights")
-        nc.gpsimd.dma_start(weights[:], w1.rearrange("(b c) m -> c b m", c=P))
+        nc.scalar.dma_start(weights[:], w1.rearrange("(b c) m -> c b m", c=P))
         bias = held.tile([P, 1], F32, name="bias")
-        nc.gpsimd.dma_start(bias[:], b1)
+        nc.scalar.dma_start(bias[:], b1)
+
+        dst, neg_dst, dst_bf = [], [], []
+        for k in range(N_CHUNKS):
+            dst.append(work.tile([P, CHUNK], F32, name="dst"))
+            nc.sync.dma_start(dst[k][:], h_dst[:, k * CHUNK : (k + 1) * CHUNK])
+            neg_dst.append(work.tile([P, CHUNK], F32, name="neg_dst"))
+            nc.scalar.activation(neg_dst[k][:], dst[k][:], ACT.Copy, scale=-1.0)
+            dst_bf.append(work.tile([P, CHUNK], BF16, name="dst_bf"))
+            nc.scalar.activation(dst_bf[k][:], dst[k][:], ACT.Copy)
 
         for k in range(N_CHUNKS):
-            edges = slice(k * CHUNK, (k + 1) * CHUNK)
             piece = offsets[:, k * OFFS_COLS : (k + 1) * OFFS_COLS]
-
-            dst = work.tile([P, CHUNK], F32, name="dst")
-            nc.sync.dma_start(dst[:], h_dst[:, edges])
-
-            neg_dst = work.tile([P, CHUNK], F32, name="neg_dst")
-            nc.gpsimd.tensor_scalar_mul(neg_dst[:], dst[:], -1.0)
-            dst_bf = work.tile([P, CHUNK], BF16, name="dst_bf")
-            nc.gpsimd.tensor_copy(dst_bf[:], dst[:])
 
             src = work.tile([P, CHUNK], F32, name="src")
             nc.vector.tensor_copy(src[:], nodes[:].indirect(piece))
             prod = work.tile([P, CHUNK], F32, name="prod")
-            nc.vector.tensor_tensor(prod[:], nodes[:].indirect(piece), dst[:], MULT)
+            nc.vector.tensor_tensor(prod[:], nodes[:].indirect(piece), dst[k][:], MULT)
             diff = work.tile([P, CHUNK], F32, name="diff")
-            nc.vector.tensor_tensor(diff[:], nodes[:].indirect(piece), neg_dst[:], ADD)
+            nc.vector.tensor_tensor(diff[:], nodes[:].indirect(piece), neg_dst[k][:], ADD)
 
             src_bf = work.tile([P, CHUNK], BF16, name="src_bf")
             nc.scalar.activation(src_bf[:], src[:], ACT.Copy)
@@ -58,11 +58,11 @@ def tile_stochasticrewiring_kernel(tc, x, h_dst, w1, b1, offs, out):
             nc.scalar.activation(diff_bf[:], diff[:], ACT.Abs)
 
             acc = psum.tile([P, CHUNK], F32, name="acc")
-            nc.tensor.matmul(acc[:], weights[:, 1, :], dst_bf[:], start=True, stop=False)
+            nc.tensor.matmul(acc[:], weights[:, 1, :], dst_bf[k][:], start=True, stop=False)
             nc.tensor.matmul(acc[:], weights[:, 0, :], src_bf[:], start=False, stop=False)
             nc.tensor.matmul(acc[:], weights[:, 3, :], prod_bf[:], start=False, stop=False)
             nc.tensor.matmul(acc[:], weights[:, 2, :], diff_bf[:], start=False, stop=True)
 
             hidden = work.tile([P, CHUNK], F32, name="hidden")
             nc.scalar.activation(hidden[:], acc[:], ACT.Relu, bias=bias[:])
-            nc.sync.dma_start(out[:, edges], hidden[:])
+            nc.sync.dma_start(out[:, k * CHUNK : (k + 1) * CHUNK], hidden[:])

@@ -17,52 +17,61 @@ FLOPS = 2 * BLOCKS * P * P * EDGES
 
 def tile_stochasticrewiring_kernel(tc, x, h_dst, w1, b1, offs, out):
     nc = tc.nc
+    chunks = [slice(k * CHUNK, (k + 1) * CHUNK) for k in range(N_CHUNKS)]
     with (
         tc.tile_pool(name="held", bufs=1) as held,
-        tc.tile_pool(name="work", bufs=N_CHUNKS) as work,
         tc.psum_pool(name="psum", bufs=N_CHUNKS) as psum,
     ):
-        offsets = held.tile([P, EDGES // 16], U16, name="offsets")
-        nc.sync.dma_start(offsets[:], offs)
         nodes = held.tile([P, NODES], F32, name="nodes")
         nc.scalar.dma_start(nodes[:], x)
+        offsets = held.tile([P, EDGES // 16], U16, name="offsets")
+        nc.sync.dma_start(offsets[:], offs)
+        dst = held.tile([P, EDGES], F32, name="dst")
+        for cols in chunks:
+            nc.sync.dma_start(dst[:, cols], h_dst[:, cols])
         weights = held.tile([P, BLOCKS, P], BF16, name="weights")
         nc.scalar.dma_start(weights[:], w1.rearrange("(b c) m -> c b m", c=P))
         bias = held.tile([P, 1], F32, name="bias")
         nc.scalar.dma_start(bias[:], b1)
 
-        dst, neg_dst, dst_bf = [], [], []
-        for k in range(N_CHUNKS):
-            dst.append(work.tile([P, CHUNK], F32, name="dst"))
-            nc.sync.dma_start(dst[k][:], h_dst[:, k * CHUNK : (k + 1) * CHUNK])
-            neg_dst.append(work.tile([P, CHUNK], F32, name="neg_dst"))
-            nc.scalar.activation(neg_dst[k][:], dst[k][:], ACT.Copy, scale=-1.0)
-            dst_bf.append(work.tile([P, CHUNK], BF16, name="dst_bf"))
-            nc.scalar.activation(dst_bf[k][:], dst[k][:], ACT.Copy)
+        def picked(k):
+            return nodes[:].indirect(offsets[:, k * OFFS_COLS : (k + 1) * OFFS_COLS])
 
-        for k in range(N_CHUNKS):
-            piece = offsets[:, k * OFFS_COLS : (k + 1) * OFFS_COLS]
+        neg_dst = held.tile([P, EDGES], F32, name="neg_dst")
+        src = held.tile([P, EDGES], F32, name="src")
+        prod = held.tile([P, EDGES], F32, name="prod")
+        diff = held.tile([P, EDGES], F32, name="diff")
+        src_bf = held.tile([P, EDGES], BF16, name="src_bf")
+        dst_bf = held.tile([P, EDGES], BF16, name="dst_bf")
+        diff_bf = held.tile([P, EDGES], BF16, name="diff_bf")
+        prod_bf = held.tile([P, EDGES], BF16, name="prod_bf")
+        hidden = held.tile([P, EDGES], F32, name="hidden")
+        acc = [psum.tile([P, CHUNK], F32, name="acc") for k in range(N_CHUNKS)]
 
-            src = work.tile([P, CHUNK], F32, name="src")
-            nc.vector.tensor_copy(src[:], nodes[:].indirect(piece))
-            prod = work.tile([P, CHUNK], F32, name="prod")
-            nc.vector.tensor_tensor(prod[:], nodes[:].indirect(piece), dst[k][:], MULT)
-            diff = work.tile([P, CHUNK], F32, name="diff")
-            nc.vector.tensor_tensor(diff[:], nodes[:].indirect(piece), neg_dst[k][:], ADD)
+        for k, cols in enumerate(chunks):
+            nc.vector.tensor_copy(src[:, cols], picked(k))
+            nc.scalar.activation(src_bf[:, cols], src[:, cols], ACT.Copy)
+            nc.tensor.matmul(acc[k][:], weights[:, 0, :], src_bf[:, cols], start=True, stop=False)
 
-            src_bf = work.tile([P, CHUNK], BF16, name="src_bf")
-            nc.scalar.activation(src_bf[:], src[:], ACT.Copy)
-            prod_bf = work.tile([P, CHUNK], BF16, name="prod_bf")
-            nc.scalar.activation(prod_bf[:], prod[:], ACT.Copy)
-            diff_bf = work.tile([P, CHUNK], BF16, name="diff_bf")
-            nc.scalar.activation(diff_bf[:], diff[:], ACT.Abs)
+        for k, cols in enumerate(chunks):
+            nc.scalar.activation(neg_dst[:, cols], dst[:, cols], ACT.Copy, scale=-1.0)
+            nc.scalar.activation(dst_bf[:, cols], dst[:, cols], ACT.Copy)
+            nc.tensor.matmul(acc[k][:], weights[:, 1, :], dst_bf[:, cols], start=False, stop=False)
 
-            acc = psum.tile([P, CHUNK], F32, name="acc")
-            nc.tensor.matmul(acc[:], weights[:, 1, :], dst_bf[k][:], start=True, stop=False)
-            nc.tensor.matmul(acc[:], weights[:, 0, :], src_bf[:], start=False, stop=False)
-            nc.tensor.matmul(acc[:], weights[:, 3, :], prod_bf[:], start=False, stop=False)
-            nc.tensor.matmul(acc[:], weights[:, 2, :], diff_bf[:], start=False, stop=True)
+        for k, cols in enumerate(chunks):
+            nc.vector.tensor_tensor(prod[:, cols], picked(k), dst[:, cols], MULT)
+            nc.scalar.activation(prod_bf[:, cols], prod[:, cols], ACT.Copy)
+            nc.tensor.matmul(acc[k][:], weights[:, 3, :], prod_bf[:, cols], start=False, stop=False)
 
-            hidden = work.tile([P, CHUNK], F32, name="hidden")
-            nc.scalar.activation(hidden[:], acc[:], ACT.Relu, bias=bias[:])
-            nc.sync.dma_start(out[:, k * CHUNK : (k + 1) * CHUNK], hidden[:])
+        def relu_and_store(k):
+            cols = chunks[k]
+            nc.scalar.activation(hidden[:, cols], acc[k][:], ACT.Relu, bias=bias[:])
+            nc.sync.dma_start(out[:, cols], hidden[:, cols])
+
+        for k, cols in enumerate(chunks):
+            nc.vector.tensor_tensor(diff[:, cols], picked(k), neg_dst[:, cols], ADD)
+            nc.scalar.activation(diff_bf[:, cols], diff[:, cols], ACT.Abs)
+            nc.tensor.matmul(acc[k][:], weights[:, 2, :], diff_bf[:, cols], start=False, stop=True)
+            if k > 0:
+                relu_and_store(k - 1)
+        relu_and_store(N_CHUNKS - 1)

@@ -10,7 +10,8 @@ EDGES = 2048
 BLOCKS = 4
 CHUNK = 512
 N_CHUNKS = EDGES // CHUNK
-OFFS_COLS = CHUNK // 16
+PIECE = 256
+STEP = 2
 
 FLOPS = 2 * BLOCKS * P * P * EDGES
 
@@ -34,14 +35,13 @@ def tile_stochasticrewiring_kernel(tc, x, h_dst, w1, b1, offs, out):
         bias = held.tile([P, 1], F32, name="bias")
         nc.scalar.dma_start(bias[:], b1)
 
-        def picked(k):
-            return nodes[:].indirect(offsets[:, k * OFFS_COLS : (k + 1) * OFFS_COLS])
+        def picked(cols):
+            return nodes[:].indirect(offsets[:, cols.start // 16 : cols.stop // 16])
 
         neg_dst = held.tile([P, EDGES], F32, name="neg_dst")
-        src = held.tile([P, EDGES], F32, name="src")
         prod = held.tile([P, EDGES], F32, name="prod")
         diff = held.tile([P, EDGES], F32, name="diff")
-        src_bf = held.tile([P, EDGES], BF16, name="src_bf")
+        src_bf = held.tile([P, EDGES, STEP], BF16, name="src_bf")
         dst_bf = held.tile([P, EDGES], BF16, name="dst_bf")
         diff_bf = held.tile([P, EDGES], BF16, name="diff_bf")
         prod_bf = held.tile([P, EDGES], BF16, name="prod_bf")
@@ -49,9 +49,10 @@ def tile_stochasticrewiring_kernel(tc, x, h_dst, w1, b1, offs, out):
         acc = [psum.tile([P, CHUNK], F32, name="acc") for k in range(N_CHUNKS)]
 
         for k, cols in enumerate(chunks):
-            nc.vector.tensor_copy(src[:, cols], picked(k))
-            nc.scalar.activation(src_bf[:, cols], src[:, cols], ACT.Copy)
-            nc.tensor.matmul(acc[k][:], weights[:, 0, :], src_bf[:, cols], start=True, stop=False)
+            for first in range(cols.start, cols.stop, PIECE):
+                piece = slice(first, first + PIECE)
+                nc.vector.tensor_copy(src_bf[:, piece, 0], picked(piece))
+            nc.tensor.matmul(acc[k][:], weights[:, 0, :], src_bf[:, cols, 0], start=True, stop=False)
 
         for k, cols in enumerate(chunks):
             nc.scalar.activation(neg_dst[:, cols], dst[:, cols], ACT.Copy, scale=-1.0)
@@ -59,7 +60,7 @@ def tile_stochasticrewiring_kernel(tc, x, h_dst, w1, b1, offs, out):
             nc.tensor.matmul(acc[k][:], weights[:, 1, :], dst_bf[:, cols], start=False, stop=False)
 
         for k, cols in enumerate(chunks):
-            nc.vector.tensor_tensor(prod[:, cols], picked(k), dst[:, cols], MULT)
+            nc.vector.tensor_tensor(prod[:, cols], picked(cols), dst[:, cols], MULT)
             nc.scalar.activation(prod_bf[:, cols], prod[:, cols], ACT.Copy)
             nc.tensor.matmul(acc[k][:], weights[:, 3, :], prod_bf[:, cols], start=False, stop=False)
 
@@ -69,7 +70,7 @@ def tile_stochasticrewiring_kernel(tc, x, h_dst, w1, b1, offs, out):
             nc.sync.dma_start(out[:, cols], hidden[:, cols])
 
         for k, cols in enumerate(chunks):
-            nc.vector.tensor_tensor(diff[:, cols], picked(k), neg_dst[:, cols], ADD)
+            nc.vector.tensor_tensor(diff[:, cols], picked(cols), neg_dst[:, cols], ADD)
             nc.scalar.activation(diff_bf[:, cols], diff[:, cols], ACT.Abs)
             nc.tensor.matmul(acc[k][:], weights[:, 2, :], diff_bf[:, cols], start=False, stop=True)
             if k > 0:

@@ -7,9 +7,9 @@ ACT = mybir.ActivationFunctionType
 P = 128
 NODES = 512
 EDGES = 2048
+SRC, DST, DIFF, PROD = 0, 1, 2, 3
 BLOCKS = 4
 CHUNK = 512
-N_CHUNKS = EDGES // CHUNK
 PIECE = 256
 STEP = 2
 
@@ -18,10 +18,11 @@ FLOPS = 2 * BLOCKS * P * P * EDGES
 
 def tile_stochasticrewiring_kernel(tc, x, h_dst, w1, b1, offs, out):
     nc = tc.nc
-    chunks = [slice(k * CHUNK, (k + 1) * CHUNK) for k in range(N_CHUNKS)]
+    chunks = [slice(first, first + CHUNK) for first in range(0, EDGES, CHUNK)]
     with (
         tc.tile_pool(name="held", bufs=1) as held,
-        tc.psum_pool(name="psum", bufs=N_CHUNKS) as psum,
+        tc.tile_pool(name="shared", bufs=len(chunks)) as shared,
+        tc.psum_pool(name="psum", bufs=EDGES // PIECE) as psum,
     ):
         nodes = held.tile([P, NODES], F32, name="nodes")
         nc.scalar.dma_start(nodes[:], x)
@@ -35,44 +36,60 @@ def tile_stochasticrewiring_kernel(tc, x, h_dst, w1, b1, offs, out):
         bias = held.tile([P, 1], F32, name="bias")
         nc.scalar.dma_start(bias[:], b1)
 
-        def picked(cols):
-            return nodes[:].indirect(offsets[:, cols.start // 16 : cols.stop // 16])
-
         neg_dst = held.tile([P, EDGES], F32, name="neg_dst")
         prod = held.tile([P, EDGES], F32, name="prod")
-        diff = held.tile([P, EDGES], F32, name="diff")
-        src_bf = held.tile([P, EDGES, STEP], BF16, name="src_bf")
         dst_bf = held.tile([P, EDGES], BF16, name="dst_bf")
         diff_bf = held.tile([P, EDGES], BF16, name="diff_bf")
         prod_bf = held.tile([P, EDGES], BF16, name="prod_bf")
         hidden = held.tile([P, EDGES], F32, name="hidden")
-        acc = [psum.tile([P, CHUNK], F32, name="acc") for k in range(N_CHUNKS)]
+        acc = [psum.tile([P, PIECE], F32, name="acc") for first in range(0, EDGES, PIECE)]
 
-        for k, cols in enumerate(chunks):
-            for first in range(cols.start, cols.stop, PIECE):
-                piece = slice(first, first + PIECE)
-                nc.vector.tensor_copy(src_bf[:, piece, 0], picked(piece))
-            nc.tensor.matmul(acc[k][:], weights[:, 0, :], src_bf[:, cols, 0], start=True, stop=False)
+        def pieces_of(chunk):
+            return [slice(first, first + PIECE) for first in range(chunk.start, chunk.stop, PIECE)]
 
-        for k, cols in enumerate(chunks):
-            nc.scalar.activation(neg_dst[:, cols], dst[:, cols], ACT.Copy, scale=-1.0)
-            nc.scalar.activation(dst_bf[:, cols], dst[:, cols], ACT.Copy)
-            nc.tensor.matmul(acc[k][:], weights[:, 1, :], dst_bf[:, cols], start=False, stop=False)
+        def picked(cols):
+            return nodes[:].indirect(offsets[:, cols.start // 16 : cols.stop // 16])
 
-        for k, cols in enumerate(chunks):
-            nc.vector.tensor_tensor(prod[:, cols], picked(cols), dst[:, cols], MULT)
-            nc.scalar.activation(prod_bf[:, cols], prod[:, cols], ACT.Copy)
-            nc.tensor.matmul(acc[k][:], weights[:, 3, :], prod_bf[:, cols], start=False, stop=False)
+        def project(block, feats_bf, cols, start=False, stop=False):
+            nc.tensor.matmul(acc[cols.start // PIECE][:], weights[:, block, :], feats_bf, start=start, stop=stop)
 
-        def relu_and_store(k):
-            cols = chunks[k]
-            nc.scalar.activation(hidden[:, cols], acc[k][:], ACT.Relu, bias=bias[:])
+        def finish(cols):
+            nc.scalar.activation(hidden[:, cols], acc[cols.start // PIECE][:], ACT.Relu, bias=bias[:])
             nc.sync.dma_start(out[:, cols], hidden[:, cols])
 
-        for k, cols in enumerate(chunks):
-            nc.vector.tensor_tensor(diff[:, cols], picked(cols), neg_dst[:, cols], ADD)
-            nc.scalar.activation(diff_bf[:, cols], diff[:, cols], ACT.Abs)
-            nc.tensor.matmul(acc[k][:], weights[:, 2, :], diff_bf[:, cols], start=False, stop=True)
-            if k > 0:
-                relu_and_store(k - 1)
-        relu_and_store(N_CHUNKS - 1)
+        def copy_block(chunk, last):
+            src_bf = shared.tile([P, CHUNK, STEP], BF16, name="src_bf", tag="four_bytes_an_edge")
+            for cols in pieces_of(chunk):
+                in_chunk = slice(cols.start - chunk.start, cols.stop - chunk.start)
+                nc.vector.tensor_copy(src_bf[:, in_chunk, 0], picked(cols))
+                if last:
+                    project(DST, dst_bf[:, cols], cols)
+                project(SRC, src_bf[:, in_chunk, 0], cols, start=not last, stop=last)
+                if last:
+                    finish(cols)
+
+        early, late = chunks[:1], chunks[1:]
+        for chunk in early:
+            copy_block(chunk, last=False)
+
+        for chunk in chunks:
+            nc.scalar.activation(neg_dst[:, chunk], dst[:, chunk], ACT.Copy, scale=-1.0)
+            nc.vector.tensor_tensor(prod[:, chunk], picked(chunk), dst[:, chunk], MULT)
+            nc.scalar.activation(prod_bf[:, chunk], prod[:, chunk], ACT.Copy)
+            for cols in pieces_of(chunk):
+                project(PROD, prod_bf[:, cols], cols, start=chunk in late)
+
+        for chunk in chunks:
+            diff = shared.tile([P, CHUNK], F32, name="diff", tag="four_bytes_an_edge")
+            nc.vector.tensor_tensor(diff[:], picked(chunk), neg_dst[:, chunk], ADD)
+            nc.scalar.activation(dst_bf[:, chunk], dst[:, chunk], ACT.Copy)
+            nc.scalar.activation(diff_bf[:, chunk], diff[:], ACT.Abs)
+            for cols in pieces_of(chunk):
+                if chunk in early:
+                    project(DST, dst_bf[:, cols], cols)
+                project(DIFF, diff_bf[:, cols], cols, stop=chunk in early)
+                if chunk in early:
+                    finish(cols)
+
+        for chunk in late:
+            copy_block(chunk, last=True)

@@ -11,6 +11,7 @@ SRC, DST, DIFF, PROD = 0, 1, 2, 3
 BLOCKS = 4
 CHUNK = 512
 PIECE = 256
+GROUPS = ((512,), (256, 256), (256, 256), (256, 192, 64))
 STEP = 2
 
 FLOPS = 2 * BLOCKS * P * P * EDGES
@@ -22,7 +23,7 @@ def tile_stochasticrewiring_kernel(tc, x, h_dst, w1, b1, offs, out):
     with (
         tc.tile_pool(name="held", bufs=1) as held,
         tc.tile_pool(name="shared", bufs=len(chunks)) as shared,
-        tc.psum_pool(name="psum", bufs=EDGES // PIECE) as psum,
+        tc.psum_pool(name="psum", bufs=sum(len(widths) for widths in GROUPS)) as psum,
     ):
         nodes = held.tile([P, NODES], F32, name="nodes")
         nc.scalar.dma_start(nodes[:], x)
@@ -42,31 +43,40 @@ def tile_stochasticrewiring_kernel(tc, x, h_dst, w1, b1, offs, out):
         diff_bf = held.tile([P, EDGES], BF16, name="diff_bf")
         prod_bf = held.tile([P, EDGES], BF16, name="prod_bf")
         hidden = held.tile([P, EDGES], F32, name="hidden")
-        acc = [psum.tile([P, PIECE], F32, name="acc") for first in range(0, EDGES, PIECE)]
 
-        def pieces_of(chunk):
-            return [slice(first, first + PIECE) for first in range(chunk.start, chunk.stop, PIECE)]
+        def groups_of(chunk):
+            widths = GROUPS[chunks.index(chunk)]
+            return [slice(chunk.start + sum(widths[:g]), chunk.start + sum(widths[: g + 1])) for g in range(len(widths))]
+
+        def pieces_of(group):
+            return [slice(first, min(first + PIECE, group.stop)) for first in range(group.start, group.stop, PIECE)]
+
+        acc = {
+            group.start: psum.tile([P, group.stop - group.start], F32, name="acc")
+            for chunk in chunks
+            for group in groups_of(chunk)
+        }
 
         def picked(cols):
             return nodes[:].indirect(offsets[:, cols.start // 16 : cols.stop // 16])
 
-        def project(block, feats_bf, cols, start=False, stop=False):
-            nc.tensor.matmul(acc[cols.start // PIECE][:], weights[:, block, :], feats_bf, start=start, stop=stop)
+        def project(block, feats_bf, group, start=False, stop=False):
+            nc.tensor.matmul(acc[group.start][:], weights[:, block, :], feats_bf, start=start, stop=stop)
 
-        def finish(cols):
-            nc.scalar.activation(hidden[:, cols], acc[cols.start // PIECE][:], ACT.Relu, bias=bias[:])
-            nc.sync.dma_start(out[:, cols], hidden[:, cols])
+        def finish(group):
+            nc.scalar.activation(hidden[:, group], acc[group.start][:], ACT.Relu, bias=bias[:])
+            nc.sync.dma_start(out[:, group], hidden[:, group])
 
         def copy_block(chunk, last):
             src_bf = shared.tile([P, CHUNK, STEP], BF16, name="src_bf", tag="four_bytes_an_edge")
-            for cols in pieces_of(chunk):
-                in_chunk = slice(cols.start - chunk.start, cols.stop - chunk.start)
-                nc.vector.tensor_copy(src_bf[:, in_chunk, 0], picked(cols))
+            for group in groups_of(chunk):
+                for cols in pieces_of(group):
+                    nc.vector.tensor_copy(src_bf[:, cols.start - chunk.start : cols.stop - chunk.start, 0], picked(cols))
                 if last:
-                    project(DST, dst_bf[:, cols], cols)
-                project(SRC, src_bf[:, in_chunk, 0], cols, start=not last, stop=last)
+                    project(DST, dst_bf[:, group], group)
+                project(SRC, src_bf[:, group.start - chunk.start : group.stop - chunk.start, 0], group, start=not last, stop=last)
                 if last:
-                    finish(cols)
+                    finish(group)
 
         early, late = chunks[:1], chunks[1:]
         for chunk in early:
@@ -76,20 +86,20 @@ def tile_stochasticrewiring_kernel(tc, x, h_dst, w1, b1, offs, out):
             nc.scalar.activation(neg_dst[:, chunk], dst[:, chunk], ACT.Copy, scale=-1.0)
             nc.vector.tensor_tensor(prod[:, chunk], picked(chunk), dst[:, chunk], MULT)
             nc.scalar.activation(prod_bf[:, chunk], prod[:, chunk], ACT.Copy)
-            for cols in pieces_of(chunk):
-                project(PROD, prod_bf[:, cols], cols, start=chunk in late)
+            for group in groups_of(chunk):
+                project(PROD, prod_bf[:, group], group, start=chunk in late)
 
         for chunk in chunks:
             diff = shared.tile([P, CHUNK], F32, name="diff", tag="four_bytes_an_edge")
             nc.vector.tensor_tensor(diff[:], picked(chunk), neg_dst[:, chunk], ADD)
             nc.scalar.activation(dst_bf[:, chunk], dst[:, chunk], ACT.Copy)
             nc.scalar.activation(diff_bf[:, chunk], diff[:], ACT.Abs)
-            for cols in pieces_of(chunk):
+            for group in groups_of(chunk):
                 if chunk in early:
-                    project(DST, dst_bf[:, cols], cols)
-                project(DIFF, diff_bf[:, cols], cols, stop=chunk in early)
+                    project(DST, dst_bf[:, group], group)
+                project(DIFF, diff_bf[:, group], group, stop=chunk in early)
                 if chunk in early:
-                    finish(cols)
+                    finish(group)
 
         for chunk in late:
             copy_block(chunk, last=True)

@@ -11,7 +11,7 @@ SRC, DST, DIFF, PROD = 0, 1, 2, 3
 BLOCKS = 4
 CHUNK = 512
 PIECE = 256
-GROUPS = ((512,), (256, 256), (256, 256), (256, 192, 64))
+GROUPS = ((512,), (512,), (256, 256), (256, 192, 64))
 STEP = 2
 
 FLOPS = 2 * BLOCKS * P * P * EDGES
@@ -78,12 +78,14 @@ def tile_stochasticrewiring_kernel(tc, x, h_dst, w1, b1, offs, out):
                 if last:
                     finish(group)
 
-        early, late = chunks[:1], chunks[1:]
+        early, late = chunks[:2], chunks[2:]
         for chunk in early:
             copy_block(chunk, last=False)
-
         for chunk in chunks:
             nc.scalar.activation(neg_dst[:, chunk], dst[:, chunk], ACT.Copy, scale=-1.0)
+            nc.scalar.activation(dst_bf[:, chunk], dst[:, chunk], ACT.Copy)
+
+        for chunk in chunks:
             nc.vector.tensor_tensor(prod[:, chunk], picked(chunk), dst[:, chunk], MULT)
             nc.scalar.activation(prod_bf[:, chunk], prod[:, chunk], ACT.Copy)
             for group in groups_of(chunk):
@@ -92,7 +94,6 @@ def tile_stochasticrewiring_kernel(tc, x, h_dst, w1, b1, offs, out):
         for chunk in chunks:
             diff = shared.tile([P, CHUNK], F32, name="diff", tag="four_bytes_an_edge")
             nc.vector.tensor_tensor(diff[:], picked(chunk), neg_dst[:, chunk], ADD)
-            nc.scalar.activation(dst_bf[:, chunk], dst[:, chunk], ACT.Copy)
             nc.scalar.activation(diff_bf[:, chunk], diff[:], ACT.Abs)
             for group in groups_of(chunk):
                 if chunk in early:

@@ -30,12 +30,14 @@ def tile_stochasticrewiring_kernel(tc, x, h_dst, w1, b1, offs, out):
         offsets = held.tile([P, EDGES // 16], U16, name="offsets")
         nc.sync.dma_start(offsets[:], offs)
         dst = held.tile([P, EDGES], F32, name="dst")
-        for cols in chunks:
+        for cols in chunks[:2]:
             nc.sync.dma_start(dst[:, cols], h_dst[:, cols])
         weights = held.tile([P, BLOCKS, P], BF16, name="weights")
-        nc.scalar.dma_start(weights[:], w1.rearrange("(b c) m -> c b m", c=P))
+        nc.sync.dma_start(weights[:], w1.rearrange("(b c) m -> c b m", c=P))
+        for cols in chunks[2:]:
+            nc.sync.dma_start(dst[:, cols], h_dst[:, cols])
         bias = held.tile([P, 1], F32, name="bias")
-        nc.scalar.dma_start(bias[:], b1)
+        nc.sync.dma_start(bias[:], b1)
 
         neg_dst = held.tile([P, EDGES], F32, name="neg_dst")
         prod = held.tile([P, EDGES], F32, name="prod")

@@ -1,7 +1,7 @@
 import concourse.mybir as mybir
 
 F32, BF16, U16 = mybir.dt.float32, mybir.dt.bfloat16, mybir.dt.uint16
-ADD, MULT = mybir.AluOpType.add, mybir.AluOpType.mult
+ADD, MAX, MULT = mybir.AluOpType.add, mybir.AluOpType.max, mybir.AluOpType.mult
 ACT = mybir.ActivationFunctionType
 
 P = 128
@@ -11,7 +11,7 @@ SRC, DST, DIFF, PROD = 0, 1, 2, 3
 BLOCKS = 4
 CHUNK = 512
 PIECE = 256
-GROUPS = ((512,), (512,), (256, 256), (256, 192, 64))
+GROUPS = ((512,), (512,), (256, 256), (256, 128, 64, 64))
 STEP = 2
 
 FLOPS = 2 * BLOCKS * P * P * EDGES
@@ -66,8 +66,12 @@ def tile_stochasticrewiring_kernel(tc, x, h_dst, w1, b1, offs, out):
             nc.tensor.matmul(acc[group.start][:], weights[:, block, :], feats_bf, start=start, stop=stop)
 
         def finish(group):
-            nc.scalar.activation(hidden[:, group], acc[group.start][:], ACT.Relu, bias=bias[:])
-            nc.sync.dma_start(out[:, group], hidden[:, group])
+            if group.stop == EDGES:
+                nc.vector.tensor_scalar(hidden[:, group], acc[group.start][:], bias[:], 0.0, ADD, MAX)
+            else:
+                nc.scalar.activation(hidden[:, group], acc[group.start][:], ACT.Relu, bias=bias[:])
+            queue = nc.scalar if group.stop == EDGES - GROUPS[-1][-1] else nc.sync
+            queue.dma_start(out[:, group], hidden[:, group])
 
         def copy_block(chunk, last):
             src_bf = shared.tile([P, CHUNK, STEP], BF16, name="src_bf", tag="four_bytes_an_edge")

@@ -41,6 +41,7 @@ def tile_stochasticrewiring_kernel(tc, x, h_dst, w1, b1, offs, out):
 
         neg_dst = held.tile([P, EDGES], F32, name="neg_dst")
         prod = held.tile([P, EDGES], F32, name="prod")
+        src_bf_early = held.tile([P, EDGES // 2], BF16, name="src_bf_early")
         dst_bf = held.tile([P, EDGES], BF16, name="dst_bf")
         diff_bf = held.tile([P, EDGES], BF16, name="diff_bf")
         prod_bf = held.tile([P, EDGES], BF16, name="prod_bf")
@@ -73,20 +74,24 @@ def tile_stochasticrewiring_kernel(tc, x, h_dst, w1, b1, offs, out):
             queue = nc.scalar if group.stop == EDGES - GROUPS[-1][-1] else nc.sync
             queue.dma_start(out[:, group], hidden[:, group])
 
-        def copy_block(chunk, last):
+        def early_copy(chunk):
+            src = shared.tile([P, CHUNK], F32, name="src", tag="four_bytes_an_edge")
+            nc.vector.tensor_copy(src[:], picked(chunk))
+            nc.scalar.activation(src_bf_early[:, chunk], src[:], ACT.Copy)
+            project(SRC, src_bf_early[:, chunk], chunk, start=True)
+
+        def late_copies(chunk):
             src_bf = shared.tile([P, CHUNK, STEP], BF16, name="src_bf", tag="four_bytes_an_edge")
             for group in groups_of(chunk):
                 for cols in pieces_of(group):
                     nc.vector.tensor_copy(src_bf[:, cols.start - chunk.start : cols.stop - chunk.start, 0], picked(cols))
-                if last:
-                    project(DST, dst_bf[:, group], group)
-                project(SRC, src_bf[:, group.start - chunk.start : group.stop - chunk.start, 0], group, start=not last, stop=last)
-                if last:
-                    finish(group)
+                project(DST, dst_bf[:, group], group)
+                project(SRC, src_bf[:, group.start - chunk.start : group.stop - chunk.start, 0], group, stop=True)
+                finish(group)
 
         early, late = chunks[:2], chunks[2:]
         for chunk in early:
-            copy_block(chunk, last=False)
+            early_copy(chunk)
         for chunk in chunks:
             nc.scalar.activation(neg_dst[:, chunk], dst[:, chunk], ACT.Copy, scale=-1.0)
             nc.scalar.activation(dst_bf[:, chunk], dst[:, chunk], ACT.Copy)
@@ -109,4 +114,4 @@ def tile_stochasticrewiring_kernel(tc, x, h_dst, w1, b1, offs, out):
                     finish(group)
 
         for chunk in late:
-            copy_block(chunk, last=True)
+            late_copies(chunk)

@@ -74,12 +74,6 @@ def tile_stochasticrewiring_kernel(tc, x, h_dst, w1, b1, offs, out):
             queue = nc.scalar if group.stop == EDGES - GROUPS[-1][-1] else nc.sync
             queue.dma_start(out[:, group], hidden[:, group])
 
-        def early_copy(chunk):
-            src = shared.tile([P, CHUNK], F32, name="src", tag="four_bytes_an_edge")
-            nc.vector.tensor_copy(src[:], picked(chunk))
-            nc.scalar.activation(src_bf_early[:, chunk], src[:], ACT.Copy)
-            project(SRC, src_bf_early[:, chunk], chunk, start=True)
-
         def late_copies(chunk):
             src_bf = shared.tile([P, CHUNK, STEP], BF16, name="src_bf", tag="four_bytes_an_edge")
             for group in groups_of(chunk):
@@ -90,11 +84,14 @@ def tile_stochasticrewiring_kernel(tc, x, h_dst, w1, b1, offs, out):
                 finish(group)
 
         early, late = chunks[:2], chunks[2:]
-        for chunk in early:
-            early_copy(chunk)
         for chunk in chunks:
             nc.scalar.activation(neg_dst[:, chunk], dst[:, chunk], ACT.Copy, scale=-1.0)
             nc.scalar.activation(dst_bf[:, chunk], dst[:, chunk], ACT.Copy)
+            if chunk in early:
+                src = shared.tile([P, CHUNK], F32, name="src", tag="four_bytes_an_edge")
+                nc.vector.tensor_copy(src[:], picked(chunk))
+                nc.scalar.activation(src_bf_early[:, chunk], src[:], ACT.Copy)
+                project(SRC, src_bf_early[:, chunk], chunk, start=True)
 
         for chunk in chunks:
             nc.vector.tensor_tensor(prod[:, chunk], picked(chunk), dst[:, chunk], MULT)

@@ -84,16 +84,22 @@ def tile_stochasticrewiring_kernel(tc, x, h_dst, w1, b1, offs, out):
                 finish(group)
 
         early, late = chunks[:2], chunks[2:]
-        for chunk in chunks:
+
+        def negate_and_round_dst(chunk):
             nc.scalar.activation(neg_dst[:, chunk], dst[:, chunk], ACT.Copy, scale=-1.0)
             nc.scalar.activation(dst_bf[:, chunk], dst[:, chunk], ACT.Copy)
-            if chunk in early:
-                src = shared.tile([P, CHUNK], F32, name="src", tag="four_bytes_an_edge")
-                nc.vector.tensor_copy(src[:], picked(chunk))
-                nc.scalar.activation(src_bf_early[:, chunk], src[:], ACT.Copy)
-                project(SRC, src_bf_early[:, chunk], chunk, start=True)
+
+        for chunk in early:
+            negate_and_round_dst(chunk)
+            src = shared.tile([P, CHUNK], F32, name="src", tag="four_bytes_an_edge")
+            nc.vector.tensor_copy(src[:], picked(chunk))
+            nc.scalar.activation(src_bf_early[:, chunk], src[:], ACT.Copy)
+            project(SRC, src_bf_early[:, chunk], chunk, start=True)
+            project(DST, dst_bf[:, chunk], chunk)
 
         for chunk in chunks:
+            if chunk in late:
+                negate_and_round_dst(chunk)
             nc.vector.tensor_tensor(prod[:, chunk], picked(chunk), dst[:, chunk], MULT)
             nc.scalar.activation(prod_bf[:, chunk], prod[:, chunk], ACT.Copy)
             for group in groups_of(chunk):
@@ -104,8 +110,6 @@ def tile_stochasticrewiring_kernel(tc, x, h_dst, w1, b1, offs, out):
             nc.vector.tensor_tensor(diff[:], picked(chunk), neg_dst[:, chunk], ADD)
             nc.scalar.activation(diff_bf[:, chunk], diff[:], ACT.Abs)
             for group in groups_of(chunk):
-                if chunk in early:
-                    project(DST, dst_bf[:, group], group)
                 project(DIFF, diff_bf[:, group], group, stop=chunk in early)
                 if chunk in early:
                     finish(group)

import concourse.mybir as mybir

F32, BF16, U16 = mybir.dt.float32, mybir.dt.bfloat16, mybir.dt.uint16
ADD, MAX, MULT = mybir.AluOpType.add, mybir.AluOpType.max, mybir.AluOpType.mult
ACT = mybir.ActivationFunctionType

P = 128
NODES = 512
EDGES = 2048
SRC, DST, DIFF, PROD = 0, 1, 2, 3
BLOCKS = 4
CHUNK = 512
PIECE = 256
GROUPS = ((512,), (512,), (256, 256), (256, 128, 64, 64))
STEP = 2

FLOPS = 2 * BLOCKS * P * P * EDGES


def tile_stochasticrewiring_kernel(tc, x, h_dst, w1, b1, offs, out):
    nc = tc.nc
    chunks = [slice(first, first + CHUNK) for first in range(0, EDGES, CHUNK)]
    with (
        tc.tile_pool(name="held", bufs=1) as held,
        tc.tile_pool(name="shared", bufs=len(chunks)) as shared,
        tc.psum_pool(name="psum", bufs=sum(len(widths) for widths in GROUPS)) as psum,
    ):
        nodes = held.tile([P, NODES], F32, name="nodes")
        nc.scalar.dma_start(nodes[:], x)
        offsets = held.tile([P, EDGES // 16], U16, name="offsets")
        nc.sync.dma_start(offsets[:], offs)
        dst = held.tile([P, EDGES], F32, name="dst")
        for cols in chunks[:2]:
            nc.sync.dma_start(dst[:, cols], h_dst[:, cols])
        weights = held.tile([P, BLOCKS, P], BF16, name="weights")
        nc.sync.dma_start(weights[:], w1.rearrange("(b c) m -> c b m", c=P))
        for cols in chunks[2:]:
            nc.sync.dma_start(dst[:, cols], h_dst[:, cols])
        bias = held.tile([P, 1], F32, name="bias")
        nc.sync.dma_start(bias[:], b1)

        neg_dst = held.tile([P, EDGES], F32, name="neg_dst")
        prod = held.tile([P, EDGES], F32, name="prod")
        src_bf_early = held.tile([P, EDGES // 2], BF16, name="src_bf_early")
        dst_bf = held.tile([P, EDGES], BF16, name="dst_bf")
        diff_bf = held.tile([P, EDGES], BF16, name="diff_bf")
        prod_bf = held.tile([P, EDGES], BF16, name="prod_bf")
        hidden = held.tile([P, EDGES], F32, name="hidden")

        def groups_of(chunk):
            widths = GROUPS[chunks.index(chunk)]
            return [slice(chunk.start + sum(widths[:g]), chunk.start + sum(widths[: g + 1])) for g in range(len(widths))]

        def pieces_of(group):
            return [slice(first, min(first + PIECE, group.stop)) for first in range(group.start, group.stop, PIECE)]

        acc = {
            group.start: psum.tile([P, group.stop - group.start], F32, name="acc")
            for chunk in chunks
            for group in groups_of(chunk)
        }

        def picked(cols):
            return nodes[:].indirect(offsets[:, cols.start // 16 : cols.stop // 16])

        def project(block, feats_bf, group, start=False, stop=False):
            nc.tensor.matmul(acc[group.start][:], weights[:, block, :], feats_bf, start=start, stop=stop)

        def finish(group):
            if group.stop == EDGES:
                nc.vector.tensor_scalar(hidden[:, group], acc[group.start][:], bias[:], 0.0, ADD, MAX)
            else:
                nc.scalar.activation(hidden[:, group], acc[group.start][:], ACT.Relu, bias=bias[:])
            queue = nc.scalar if group.stop == EDGES - GROUPS[-1][-1] else nc.sync
            queue.dma_start(out[:, group], hidden[:, group])

        def late_copies(chunk):
            src_bf = shared.tile([P, CHUNK, STEP], BF16, name="src_bf", tag="four_bytes_an_edge")
            for group in groups_of(chunk):
                for cols in pieces_of(group):
                    nc.vector.tensor_copy(src_bf[:, cols.start - chunk.start : cols.stop - chunk.start, 0], picked(cols))
                project(DST, dst_bf[:, group], group)
                project(SRC, src_bf[:, group.start - chunk.start : group.stop - chunk.start, 0], group, stop=True)
                finish(group)

        early, late = chunks[:2], chunks[2:]

        def negate_and_round_dst(chunk):
            nc.scalar.activation(neg_dst[:, chunk], dst[:, chunk], ACT.Copy, scale=-1.0)
            nc.scalar.activation(dst_bf[:, chunk], dst[:, chunk], ACT.Copy)

        for chunk in early:
            negate_and_round_dst(chunk)
            src = shared.tile([P, CHUNK], F32, name="src", tag="four_bytes_an_edge")
            nc.vector.tensor_copy(src[:], picked(chunk))
            nc.scalar.activation(src_bf_early[:, chunk], src[:], ACT.Copy)
            project(SRC, src_bf_early[:, chunk], chunk, start=True)
            project(DST, dst_bf[:, chunk], chunk)

        for chunk in chunks:
            if chunk in late:
                negate_and_round_dst(chunk)
            nc.vector.tensor_tensor(prod[:, chunk], picked(chunk), dst[:, chunk], MULT)
            nc.scalar.activation(prod_bf[:, chunk], prod[:, chunk], ACT.Copy)
            for group in groups_of(chunk):
                project(PROD, prod_bf[:, group], group, start=chunk in late)

        for chunk in chunks:
            diff = shared.tile([P, CHUNK], F32, name="diff", tag="four_bytes_an_edge")
            nc.vector.tensor_tensor(diff[:], picked(chunk), neg_dst[:, chunk], ADD)
            nc.scalar.activation(diff_bf[:, chunk], diff[:], ACT.Abs)
            for group in groups_of(chunk):
                project(DIFF, diff_bf[:, group], group, stop=chunk in early)
                if chunk in early:
                    finish(group)

        for chunk in late:
            late_copies(chunk)
